import numpy as np
import ml_dtypes


def mxq(x, axis, fmt="e4m3"):
    dtype, down = {"e4m3": (ml_dtypes.float8_e4m3fn, 7), "e5m2": (ml_dtypes.float8_e5m2, 14)}[fmt]
    v = np.moveaxis(np.asarray(x, np.float32).astype(ml_dtypes.bfloat16).astype(np.float64), axis, -1)
    blocks = v.reshape(v.shape[:-1] + (-1, 32))
    amax = np.abs(blocks).max(-1, keepdims=True)
    byte = np.maximum(np.where(amax > 0, np.frexp(amax)[1] - 1 + 127, 0) - down, 1)
    scale = np.exp2(byte - 127.0)
    codes = (blocks / scale).astype(np.float32).astype(dtype).astype(np.float64)
    return np.moveaxis((codes * scale).reshape(v.shape), -1, axis)


WIDE = False


def mx_kscale(k):
    if not WIDE:
        return np.ones(k)
    levels = np.array([10, -10, 5, -5, 0])
    a = np.random.permutation(np.resize(levels, k // 512 * 4)).reshape(k // 512, 4)
    idx = np.arange(k)
    return np.exp2(a[idx // 512, idx % 128 // 32])


BF16 = ml_dtypes.bfloat16


def bf(x):
    return np.asarray(x, np.float32).astype(BF16)


def f64(x):
    return np.asarray(x).astype(np.float64)


B, IN, OUT = 4096, 512, 512


def sigmoid(v):
    return 1.0 / (1.0 + np.exp(-v))


def setup_inputs():
    s, t = mx_kscale(IN), mx_kscale(OUT)
    return {
        "x": bf(np.random.standard_normal((B, IN)) * s),
        "hx": bf(np.random.standard_normal((B, OUT)) * t),
        "cy": bf(np.random.standard_normal((B, OUT)) * 0.5),
        "w_ih_o": bf(np.random.standard_normal((OUT, IN)) * 0.7 / np.sqrt(IN) / s),
        "w_hh_o": bf(np.random.standard_normal((OUT, OUT)) * 0.7 / np.sqrt(OUT) / t),
        "w_po": bf(np.random.standard_normal((OUT, OUT)) * 1.5 / np.sqrt(OUT)),
        "b_ih_o": bf(np.random.standard_normal(OUT) * 0.3),
        "b_hh_o": bf(np.random.standard_normal(OUT) * 0.3),
    }


def reference(x, hx, cy, w_ih_o, w_hh_o, w_po, b_ih_o, b_hh_o):
    c = f64(cy)
    o_g = (mxq(f64(x), 1, "e4m3") @ mxq(f64(w_ih_o), 1, "e4m3").T) + f64(b_ih_o) + (mxq(f64(hx), 1, "e4m3") @ mxq(f64(w_hh_o), 1, "e4m3").T) + f64(b_hh_o)
    o_g = sigmoid(o_g + (mxq(c, 1, "e4m3") @ mxq(f64(w_po), 1, "e4m3").T))
    return o_g * np.tanh(c)

@@ -1,0 +1,177 @@
+from contextlib import ExitStack
+
+import concourse.mybir as mybir
+from concourse.masks import make_identity
+
+F32 = mybir.dt.float32
+BF16 = mybir.dt.bfloat16
+U32 = mybir.dt.uint32
+U8 = mybir.dt.uint8
+FP8X4 = mybir.dt.float8_e4m3fn_x4
+ACT = mybir.ActivationFunctionType
+ALU = mybir.AluOpType
+
+P = 128
+PACK = 4
+HALVES = 2
+PAIR = 2
+BATCH, K, N_OUT = 4096, 512, 512
+ROW_TILES = BATCH // P
+ROUNDS = ROW_TILES // PAIR
+WEIGHT_PAIRS = N_OUT // (PAIR * P)
+OPERANDS = 3
+CY = 2
+
+FLOPS = 2 * BATCH * K * N_OUT * OPERANDS
+
+
+def tile_ircnn_lstmcell_pb_t_kernel(
+    tc, x, hx, cy, w_ih_o, w_hh_o, w_po, b_ih_o, b_hh_o, out
+):
+    nc = tc.nc
+    acts = [a.rearrange("(p t) k -> p t k", t=ROW_TILES) for a in (x, hx, cy)]
+    out_rows = out.rearrange("(p t) n -> p t n", t=ROW_TILES)
+    weights = [w.rearrange("(r p) k -> p r k", p=P) for w in (w_ih_o, w_hh_o, w_po)]
+
+    with ExitStack() as ctx:
+        consts = ctx.enter_context(tc.tile_pool(name="consts", bufs=1))
+        resident = ctx.enter_context(tc.tile_pool(name="resident", bufs=1))
+        grouped_pool = ctx.enter_context(tc.tile_pool(name="grouped", bufs=2))
+        mx_pool = ctx.enter_context(tc.tile_pool(name="mx", bufs=3))
+        tanh_pool = ctx.enter_context(tc.tile_pool(name="tanh", bufs=3))
+        gate_pool = ctx.enter_context(tc.tile_pool(name="gate", bufs=8))
+        banks = ctx.enter_context(tc.psum_pool(name="banks", bufs=4))
+        sums = ctx.enter_context(tc.psum_pool(name="sums", bufs=4))
+        ctx.enter_context(tc.manual_schedule())
+
+        ident = consts.tile([P, P], F32)
+        make_identity(nc, ident[:])
+        ones = consts.tile([P, P], BF16)
+        nc.vector.memset(ones[:], 1.0)
+        bias_rows = consts.tile([P, N_OUT], BF16)
+        nc.vector.memset(bias_rows[:], 0.0)
+        nc.scalar.dma_start(out=bias_rows[0:1, :], in_=b_ih_o.rearrange("(o n) -> o n", o=1))
+        nc.scalar.dma_start(out=bias_rows[1:2, :], in_=b_hh_o.rearrange("(o n) -> o n", o=1))
+        warm = consts.tile([P, 1], F32)
+        nc.vector.memset(warm[:], 0.0)
+        warm_out = consts.tile([P, 1], F32)
+        nc.scalar.activation(out=warm_out[:], in_=warm[:], func=ACT.Sigmoid)
+
+        w_raw = [resident.tile([P, N_OUT // P, K], BF16, name="w_raw%d" % i) for i in range(OPERANDS)]
+        rows = [
+            [resident.tile([P, PAIR, K], BF16, name="rows%d_%d" % (i, g)) for g in range(ROUNDS)]
+            for i in range(OPERANDS)
+        ]
+
+        def load_rows(i, g):
+            nc.sync.dma_start(out=rows[i][g][:], in_=acts[i][:, g * PAIR : (g + 1) * PAIR, :])
+
+        for i in range(OPERANDS):
+            nc.sync.dma_start(out=w_raw[i][:], in_=weights[i])
+            load_rows(i, 0)
+        for g in range(1, ROUNDS):
+            for i in range(OPERANDS):
+                load_rows(i, g)
+
+        def transpose_pair(rows_bf16, grouped, copy):
+            bank = banks.tile([P, PAIR, HALVES, P], F32, name="bank")
+            words = rows_bf16.bitcast(F32)
+            for j in range(PAIR):
+                for u in range(HALVES):
+                    nc.tensor.transpose(bank[:, j, u, :], words[:, j, u * P : (u + 1) * P], ident[:])
+            copy(out=grouped.bitcast(F32), in_=bank[:].rearrange("p j u r -> p j r u"))
+
+        grouped = {}
+        codes = {}
+        scales = {}
+        acc = {}
+        gate = {}
+        tanh_c = {}
+
+        def regroup(i, g):
+            grouped[i, g] = grouped_pool.tile([P, PAIR, P, PACK], BF16, name="grouped%d" % i, align_bytes=64)
+            copy = nc.vector.tensor_copy if i == CY else nc.scalar.copy
+            transpose_pair(rows[i][g][:], grouped[i, g][:], copy)
+
+        def quantise(i, g):
+            codes[i, g] = mx_pool.tile([P, PAIR * P], U32, name="codes%d" % i, align_bytes=64)
+            scales[i, g] = mx_pool.tile([P, PAIR * P], U8, name="scales%d" % i, align_bytes=64)
+            nc.vector.quantize_mx(
+                out=codes[i, g][:].bitcast(FP8X4),
+                scales=scales[i, g][:],
+                in_=grouped[i, g][:].rearrange("p j r t -> p (j r t)"),
+            )
+
+        def multiply(g):
+            for j in range(PAIR):
+                acc[g, j] = sums.tile([P, N_OUT], F32, name="acc")
+                tile_cols = slice(j * P, (j + 1) * P)
+                for i in range(OPERANDS):
+                    nc.tensor.matmul_mx(
+                        out=acc[g, j][:],
+                        lhsT=codes[i, g][:, tile_cols].bitcast(FP8X4),
+                        lhsT_scale=scales[i, g][:, tile_cols],
+                        rhs=w_codes[i][:].bitcast(FP8X4),
+                        rhs_scale=w_scales[i][:],
+                        start=(i == 0),
+                        stop=(i == OPERANDS - 1),
+                    )
+
+        def add_bias(g):
+            gate[g] = gate_pool.tile([P, PAIR, N_OUT], F32, name="gate")
+            for j in range(PAIR):
+                nc.vector.tensor_tensor(out=gate[g][:, j, :], in0=acc[g, j][:], in1=bias[:], op=ALU.add)
+
+        def tanh_of_cell(g):
+            tanh_c[g] = tanh_pool.tile([P, PAIR, N_OUT], F32, name="tanh_c")
+            nc.scalar.activation(out=tanh_c[g][:], in_=rows[CY][g][:], func=ACT.Tanh)
+
+        def sigmoid(g):
+            nc.scalar.activation(out=gate[g][:], in_=gate[g][:], func=ACT.Sigmoid)
+
+        def product_and_store(g):
+            nc.vector.tensor_tensor(out=gate[g][:], in0=gate[g][:], in1=tanh_c[g][:], op=ALU.mult)
+            nc.sync.dma_start(out=out_rows[:, g * PAIR : (g + 1) * PAIR, :], in_=gate[g][:])
+
+        w_codes = []
+        w_scales = []
+        for i in range(OPERANDS):
+            w_grouped = resident.tile([P, N_OUT // P, P, PACK], BF16, name="w_grouped%d" % i, align_bytes=64)
+            for h in range(WEIGHT_PAIRS):
+                tiles = slice(h * PAIR, (h + 1) * PAIR)
+                copy = nc.vector.tensor_copy if h == 1 else nc.scalar.copy
+                transpose_pair(w_raw[i][:, tiles, :], w_grouped[:, tiles, :, :], copy)
+            regroup(i, 0)
+            w_codes.append(resident.tile([P, N_OUT], U32, name="w_codes%d" % i, align_bytes=64))
+            w_scales.append(resident.tile([P, N_OUT], U8, name="w_scales%d" % i, align_bytes=64))
+            nc.vector.quantize_mx(
+                out=w_codes[i][:].bitcast(FP8X4),
+                scales=w_scales[i][:],
+                in_=w_grouped[:].rearrange("p j r t -> p (j r t)"),
+            )
+            quantise(i, 0)
+
+        bias_sum = sums.tile([P, N_OUT], F32, name="acc")
+        nc.tensor.matmul(out=bias_sum[:], lhsT=ones[:], rhs=bias_rows[:], start=True, stop=True)
+        bias = consts.tile([P, N_OUT], F32)
+        nc.vector.tensor_copy(out=bias[:], in_=bias_sum[:])
+
+        for i in range(OPERANDS):
+            regroup(i, 1)
+
+        for g in range(ROUNDS + 1):
+            if g + 1 < ROUNDS:
+                for i in range(OPERANDS):
+                    quantise(i, g + 1)
+            if g >= 1:
+                sigmoid(g - 1)
+            if g + 2 < ROUNDS:
+                for i in range(OPERANDS):
+                    regroup(i, g + 2)
+            if g < ROUNDS:
+                multiply(g)
+                tanh_of_cell(g)
+            if g >= 1:
+                product_and_store(g - 1)
+            if g < ROUNDS:
+                add_bias(g)

@@ -90,7 +90,7 @@ def tile_ircnn_lstmcell_pb_t_kernel(
 
         def regroup(i, g):
             grouped[i, g] = grouped_pool.tile([P, PAIR, P, PACK], BF16, name="grouped%d" % i, align_bytes=64)
-            copy = nc.vector.tensor_copy if i == CY else nc.scalar.copy
+            copy = nc.scalar.copy if (OPERANDS * g + i) % 2 == 0 else nc.vector.tensor_copy
             transpose_pair(rows[i][g][:], grouped[i, g][:], copy)
 
         def quantise(i, g):
@@ -130,7 +130,10 @@ def tile_ircnn_lstmcell_pb_t_kernel(
             nc.scalar.activation(out=gate[g][:], in_=gate[g][:], func=ACT.Sigmoid)
 
         def product_and_store(g):
-            nc.vector.tensor_tensor(out=gate[g][:], in0=gate[g][:], in1=tanh_c[g][:], op=ALU.mult)
+            for j in range(PAIR):
+                nc.gpsimd.tensor_tensor(
+                    out=gate[g][:, j, :], in0=gate[g][:, j, :], in1=tanh_c[g][:, j, :], op=ALU.mult
+                )
             nc.sync.dma_start(out=out_rows[:, g * PAIR : (g + 1) * PAIR, :], in_=gate[g][:])
 
         w_codes = []

@@ -38,7 +38,7 @@ def tile_ircnn_lstmcell_pb_t_kernel(
         resident = ctx.enter_context(tc.tile_pool(name="resident", bufs=1))
         grouped_pool = ctx.enter_context(tc.tile_pool(name="grouped", bufs=2))
         mx_pool = ctx.enter_context(tc.tile_pool(name="mx", bufs=3))
-        tanh_pool = ctx.enter_context(tc.tile_pool(name="tanh", bufs=3))
+        tanh_pool = ctx.enter_context(tc.tile_pool(name="tanh", bufs=4))
         gate_pool = ctx.enter_context(tc.tile_pool(name="gate", bufs=8))
         banks = ctx.enter_context(tc.psum_pool(name="banks", bufs=4))
         sums = ctx.enter_context(tc.psum_pool(name="sums", bufs=4))
@@ -90,7 +90,7 @@ def tile_ircnn_lstmcell_pb_t_kernel(
 
         def regroup(i, g):
             grouped[i, g] = grouped_pool.tile([P, PAIR, P, PACK], BF16, name="grouped%d" % i, align_bytes=64)
-            copy = nc.scalar.copy if (OPERANDS * g + i) % 2 == 0 else nc.vector.tensor_copy
+            copy = nc.vector.tensor_copy if i == CY else nc.scalar.copy
             transpose_pair(rows[i][g][:], grouped[i, g][:], copy)
 
         def quantise(i, g):
@@ -127,11 +127,12 @@ def tile_ircnn_lstmcell_pb_t_kernel(
             nc.scalar.activation(out=tanh_c[g][:], in_=rows[CY][g][:], func=ACT.Tanh)
 
         def sigmoid(g):
-            nc.scalar.activation(out=gate[g][:], in_=gate[g][:], func=ACT.Sigmoid)
+            for j in range(PAIR):
+                nc.scalar.activation(out=gate[g][:, j, :], in_=gate[g][:, j, :], func=ACT.Sigmoid)
 
         def product_and_store(g):
-            for j in range(PAIR):
-                nc.gpsimd.tensor_tensor(
+            for j, engine in enumerate((nc.gpsimd, nc.vector)):
+                engine.tensor_tensor(
                     out=gate[g][:, j, :], in0=gate[g][:, j, :], in1=tanh_c[g][:, j, :], op=ALU.mult
                 )
             nc.sync.dma_start(out=out_rows[:, g * PAIR : (g + 1) * PAIR, :], in_=gate[g][:])
@@ -162,11 +163,13 @@ def tile_ircnn_lstmcell_pb_t_kernel(
         for i in range(OPERANDS):
             regroup(i, 1)
 
-        for g in range(ROUNDS + 1):
+        for g in range(ROUNDS + 2):
             if g + 1 < ROUNDS:
                 for i in range(OPERANDS):
                     quantise(i, g + 1)
-            if g >= 1:
+            if g >= 2:
+                product_and_store(g - 2)
+            if g >= 1 and g <= ROUNDS:
                 sigmoid(g - 1)
             if g + 2 < ROUNDS:
                 for i in range(OPERANDS):
@@ -174,7 +177,4 @@ def tile_ircnn_lstmcell_pb_t_kernel(
             if g < ROUNDS:
                 multiply(g)
                 tanh_of_cell(g)
-            if g >= 1:
-                product_and_store(g - 1)
-            if g < ROUNDS:
                 add_bias(g)

@@ -20,7 +20,9 @@ ROW_TILES = BATCH // P
 ROUNDS = ROW_TILES // PAIR
 WEIGHT_PAIRS = N_OUT // (PAIR * P)
 OPERANDS = 3
+HX = 1
 CY = 2
+VECTOR_HELPS_EVERY = 4
 
 FLOPS = 2 * BATCH * K * N_OUT * OPERANDS
 
@@ -31,7 +33,7 @@ def tile_ircnn_lstmcell_pb_t_kernel(
     nc = tc.nc
     acts = [a.rearrange("(p t) k -> p t k", t=ROW_TILES) for a in (x, hx, cy)]
     out_rows = out.rearrange("(p t) n -> p t n", t=ROW_TILES)
-    weights = [w.rearrange("(r p) k -> p r k", p=P) for w in (w_ih_o, w_hh_o, w_po)]
+    weights = [w.rearrange("(c r) k -> c r k", r=N_OUT // P) for w in (w_ih_o, w_hh_o, w_po)]
 
     with ExitStack() as ctx:
         consts = ctx.enter_context(tc.tile_pool(name="consts", bufs=1))
@@ -73,13 +75,13 @@ def tile_ircnn_lstmcell_pb_t_kernel(
             for i in range(OPERANDS):
                 load_rows(i, g)
 
-        def transpose_pair(rows_bf16, grouped, copy):
+        def transpose_pair(rows_bf16):
             bank = banks.tile([P, PAIR, HALVES, P], F32, name="bank")
             words = rows_bf16.bitcast(F32)
             for j in range(PAIR):
                 for u in range(HALVES):
                     nc.tensor.transpose(bank[:, j, u, :], words[:, j, u * P : (u + 1) * P], ident[:])
-            copy(out=grouped.bitcast(F32), in_=bank[:].rearrange("p j u r -> p j r u"))
+            return bank
 
         grouped = {}
         codes = {}
@@ -90,8 +92,10 @@ def tile_ircnn_lstmcell_pb_t_kernel(
 
         def regroup(i, g):
             grouped[i, g] = grouped_pool.tile([P, PAIR, P, PACK], BF16, name="grouped%d" % i, align_bytes=64)
-            copy = nc.vector.tensor_copy if i == CY else nc.scalar.copy
-            transpose_pair(rows[i][g][:], grouped[i, g][:], copy)
+            vector_helps = g % VECTOR_HELPS_EVERY == VECTOR_HELPS_EVERY - 1
+            copy = nc.vector.tensor_copy if i == CY or (i == HX and vector_helps) else nc.scalar.copy
+            bank = transpose_pair(rows[i][g][:])
+            copy(out=grouped[i, g][:].bitcast(F32), in_=bank[:].rearrange("p j u r -> p j r u"))
 
         def quantise(i, g):
             codes[i, g] = mx_pool.tile([P, PAIR * P], U32, name="codes%d" % i, align_bytes=64)
@@ -135,23 +139,23 @@ def tile_ircnn_lstmcell_pb_t_kernel(
                 engine.tensor_tensor(
                     out=gate[g][:, j, :], in0=gate[g][:, j, :], in1=tanh_c[g][:, j, :], op=ALU.mult
                 )
-            nc.sync.dma_start(out=out_rows[:, g * PAIR : (g + 1) * PAIR, :], in_=gate[g][:])
+                nc.sync.dma_start(out=out_rows[:, g * PAIR + j, :], in_=gate[g][:, j, :])
 
         w_codes = []
         w_scales = []
         for i in range(OPERANDS):
-            w_grouped = resident.tile([P, N_OUT // P, P, PACK], BF16, name="w_grouped%d" % i, align_bytes=64)
+            w_grouped = resident.tile([P, N_OUT, PACK], BF16, name="w_grouped%d" % i, align_bytes=64)
+            w_words = w_grouped[:].bitcast(F32).rearrange("p (c h j) u -> p c h j u", h=WEIGHT_PAIRS, j=PAIR)
             for h in range(WEIGHT_PAIRS):
-                tiles = slice(h * PAIR, (h + 1) * PAIR)
-                copy = nc.vector.tensor_copy if h == 1 else nc.scalar.copy
-                transpose_pair(w_raw[i][:, tiles, :], w_grouped[:, tiles, :, :], copy)
+                bank = transpose_pair(w_raw[i][:, h * PAIR : (h + 1) * PAIR, :])
+                nc.scalar.copy(out=w_words[:, :, h, :, :], in_=bank[:].rearrange("p j u c -> p c j u"))
             regroup(i, 0)
             w_codes.append(resident.tile([P, N_OUT], U32, name="w_codes%d" % i, align_bytes=64))
             w_scales.append(resident.tile([P, N_OUT], U8, name="w_scales%d" % i, align_bytes=64))
             nc.vector.quantize_mx(
                 out=w_codes[i][:].bitcast(FP8X4),
                 scales=w_scales[i][:],
-                in_=w_grouped[:].rearrange("p j r t -> p (j r t)"),
+                in_=w_grouped[:].rearrange("p n t -> p (n t)"),
             )
             quantise(i, 0)
 

@@ -20,9 +20,9 @@ ROW_TILES = BATCH // P
 ROUNDS = ROW_TILES // PAIR
 WEIGHT_PAIRS = N_OUT // (PAIR * P)
 OPERANDS = 3
+X = 0
 HX = 1
 CY = 2
-VECTOR_HELPS_EVERY = 4
 
 FLOPS = 2 * BATCH * K * N_OUT * OPERANDS
 
@@ -33,14 +33,14 @@ def tile_ircnn_lstmcell_pb_t_kernel(
     nc = tc.nc
     acts = [a.rearrange("(p t) k -> p t k", t=ROW_TILES) for a in (x, hx, cy)]
     out_rows = out.rearrange("(p t) n -> p t n", t=ROW_TILES)
-    weights = [w.rearrange("(c r) k -> c r k", r=N_OUT // P) for w in (w_ih_o, w_hh_o, w_po)]
+    weights = [w.rearrange("(h c j) k -> h c j k", h=WEIGHT_PAIRS, j=PAIR) for w in (w_ih_o, w_hh_o, w_po)]
 
     with ExitStack() as ctx:
         consts = ctx.enter_context(tc.tile_pool(name="consts", bufs=1))
         resident = ctx.enter_context(tc.tile_pool(name="resident", bufs=1))
         grouped_pool = ctx.enter_context(tc.tile_pool(name="grouped", bufs=2))
         mx_pool = ctx.enter_context(tc.tile_pool(name="mx", bufs=3))
-        tanh_pool = ctx.enter_context(tc.tile_pool(name="tanh", bufs=4))
+        tanh_pool = ctx.enter_context(tc.tile_pool(name="tanh", bufs=8))
         gate_pool = ctx.enter_context(tc.tile_pool(name="gate", bufs=8))
         banks = ctx.enter_context(tc.psum_pool(name="banks", bufs=4))
         sums = ctx.enter_context(tc.psum_pool(name="sums", bufs=4))
@@ -59,7 +59,10 @@ def tile_ircnn_lstmcell_pb_t_kernel(
         warm_out = consts.tile([P, 1], F32)
         nc.scalar.activation(out=warm_out[:], in_=warm[:], func=ACT.Sigmoid)
 
-        w_raw = [resident.tile([P, N_OUT // P, K], BF16, name="w_raw%d" % i) for i in range(OPERANDS)]
+        w_raw = [
+            [resident.tile([P, PAIR, K], BF16, name="w_raw%d_%d" % (i, h)) for h in range(WEIGHT_PAIRS)]
+            for i in range(OPERANDS)
+        ]
         rows = [
             [resident.tile([P, PAIR, K], BF16, name="rows%d_%d" % (i, g)) for g in range(ROUNDS)]
             for i in range(OPERANDS)
@@ -68,12 +71,22 @@ def tile_ircnn_lstmcell_pb_t_kernel(
         def load_rows(i, g):
             nc.sync.dma_start(out=rows[i][g][:], in_=acts[i][:, g * PAIR : (g + 1) * PAIR, :])
 
-        for i in range(OPERANDS):
-            nc.sync.dma_start(out=w_raw[i][:], in_=weights[i])
-            load_rows(i, 0)
+        def load_weights(i):
+            for h in range(WEIGHT_PAIRS):
+                nc.sync.dma_start(out=w_raw[i][h][:], in_=weights[i][h])
+
+        load_rows(CY, 0)
+        load_weights(CY)
+        load_rows(CY, 1)
+        load_weights(X)
+        load_rows(X, 0)
+        load_weights(HX)
+        load_rows(HX, 0)
         for g in range(1, ROUNDS):
-            for i in range(OPERANDS):
-                load_rows(i, g)
+            if g + 1 < ROUNDS:
+                load_rows(CY, g + 1)
+            load_rows(X, g)
+            load_rows(HX, g)
 
         def transpose_pair(rows_bf16):
             bank = banks.tile([P, PAIR, HALVES, P], F32, name="bank")
@@ -90,10 +103,8 @@ def tile_ircnn_lstmcell_pb_t_kernel(
         gate = {}
         tanh_c = {}
 
-        def regroup(i, g):
+        def regroup(i, g, copy):
             grouped[i, g] = grouped_pool.tile([P, PAIR, P, PACK], BF16, name="grouped%d" % i, align_bytes=64)
-            vector_helps = g % VECTOR_HELPS_EVERY == VECTOR_HELPS_EVERY - 1
-            copy = nc.vector.tensor_copy if i == CY or (i == HX and vector_helps) else nc.scalar.copy
             bank = transpose_pair(rows[i][g][:])
             copy(out=grouped[i, g][:].bitcast(F32), in_=bank[:].rearrange("p j u r -> p j r u"))
 
@@ -110,15 +121,15 @@ def tile_ircnn_lstmcell_pb_t_kernel(
             for j in range(PAIR):
                 acc[g, j] = sums.tile([P, N_OUT], F32, name="acc")
                 tile_cols = slice(j * P, (j + 1) * P)
-                for i in range(OPERANDS):
+                for i in (CY, X, HX):
                     nc.tensor.matmul_mx(
                         out=acc[g, j][:],
                         lhsT=codes[i, g][:, tile_cols].bitcast(FP8X4),
                         lhsT_scale=scales[i, g][:, tile_cols],
                         rhs=w_codes[i][:].bitcast(FP8X4),
                         rhs_scale=w_scales[i][:],
-                        start=(i == 0),
-                        stop=(i == OPERANDS - 1),
+                        start=(i == CY),
+                        stop=(i == HX),
                     )
 
         def add_bias(g):
@@ -141,44 +152,69 @@ def tile_ircnn_lstmcell_pb_t_kernel(
                 )
                 nc.sync.dma_start(out=out_rows[:, g * PAIR + j, :], in_=gate[g][:, j, :])
 
-        w_codes = []
-        w_scales = []
-        for i in range(OPERANDS):
-            w_grouped = resident.tile([P, N_OUT, PACK], BF16, name="w_grouped%d" % i, align_bytes=64)
-            w_words = w_grouped[:].bitcast(F32).rearrange("p (c h j) u -> p c h j u", h=WEIGHT_PAIRS, j=PAIR)
-            for h in range(WEIGHT_PAIRS):
-                bank = transpose_pair(w_raw[i][:, h * PAIR : (h + 1) * PAIR, :])
-                nc.scalar.copy(out=w_words[:, :, h, :, :], in_=bank[:].rearrange("p j u c -> p c j u"))
-            regroup(i, 0)
-            w_codes.append(resident.tile([P, N_OUT], U32, name="w_codes%d" % i, align_bytes=64))
-            w_scales.append(resident.tile([P, N_OUT], U8, name="w_scales%d" % i, align_bytes=64))
+        w_grouped = [
+            resident.tile([P, N_OUT, PACK], BF16, name="w_grouped%d" % i, align_bytes=64) for i in range(OPERANDS)
+        ]
+        w_codes = [resident.tile([P, N_OUT], U32, name="w_codes%d" % i, align_bytes=64) for i in range(OPERANDS)]
+        w_scales = [resident.tile([P, N_OUT], U8, name="w_scales%d" % i, align_bytes=64) for i in range(OPERANDS)]
+
+        def regroup_weights(i, h, copy):
+            half = w_grouped[i][:].bitcast(F32)[:, h * PAIR * P : (h + 1) * PAIR * P, :]
+            bank = transpose_pair(w_raw[i][h][:])
+            copy(
+                out=half.rearrange("p (c j) u -> p c j u", j=PAIR),
+                in_=bank[:].rearrange("p j u c -> p c j u"),
+            )
+
+        def quantise_weights(i):
             nc.vector.quantize_mx(
                 out=w_codes[i][:].bitcast(FP8X4),
                 scales=w_scales[i][:],
-                in_=w_grouped[:].rearrange("p n t -> p (n t)"),
+                in_=w_grouped[i][:].rearrange("p n t -> p (n t)"),
             )
-            quantise(i, 0)
 
+        tanh_of_cell(0)
+        regroup(CY, 0, nc.vector.tensor_copy)
         bias_sum = sums.tile([P, N_OUT], F32, name="acc")
         nc.tensor.matmul(out=bias_sum[:], lhsT=ones[:], rhs=bias_rows[:], start=True, stop=True)
         bias = consts.tile([P, N_OUT], F32)
         nc.vector.tensor_copy(out=bias[:], in_=bias_sum[:])
-
-        for i in range(OPERANDS):
-            regroup(i, 1)
+        regroup_weights(CY, 0, nc.vector.tensor_copy)
+        quantise(CY, 0)
+        regroup_weights(CY, 1, nc.scalar.copy)
+        tanh_of_cell(1)
+        regroup(CY, 1, nc.vector.tensor_copy)
+        quantise_weights(CY)
+        regroup_weights(X, 0, nc.vector.tensor_copy)
+        regroup_weights(X, 1, nc.scalar.copy)
+        quantise(CY, 1)
+        regroup(X, 0, nc.scalar.copy)
+        quantise_weights(X)
+        regroup_weights(HX, 0, nc.vector.tensor_copy)
+        quantise(X, 0)
+        regroup_weights(HX, 1, nc.scalar.copy)
+        regroup(HX, 0, nc.vector.tensor_copy)
+        quantise_weights(HX)
+        tanh_of_cell(2)
+        quantise(HX, 0)
+        regroup(X, 1, nc.scalar.copy)
+        regroup(HX, 1, nc.vector.tensor_copy)
 
         for g in range(ROUNDS + 2):
-            if g + 1 < ROUNDS:
-                for i in range(OPERANDS):
-                    quantise(i, g + 1)
             if g >= 2:
                 product_and_store(g - 2)
+            if g + 1 < ROUNDS:
+                for i in (CY, X, HX):
+                    if (i, g + 1) not in codes:
+                        quantise(i, g + 1)
+            if g + 3 < ROUNDS:
+                tanh_of_cell(g + 3)
             if g >= 1 and g <= ROUNDS:
                 sigmoid(g - 1)
-            if g + 2 < ROUNDS:
-                for i in range(OPERANDS):
-                    regroup(i, g + 2)
             if g < ROUNDS:
                 multiply(g)
-                tanh_of_cell(g)
                 add_bias(g)
+            if g + 2 < ROUNDS:
+                regroup(CY, g + 2, nc.vector.tensor_copy)
+                regroup(X, g + 2, nc.scalar.copy)
+                regroup(HX, g + 2, nc.scalar.copy)

@@ -132,10 +132,17 @@ def tile_ircnn_lstmcell_pb_t_kernel(
                         stop=(i == HX),
                     )
 
+        def pieces(g, j):
+            width = N_OUT // 2 if (g, j) == (ROUNDS - 1, PAIR - 1) else N_OUT
+            return [slice(n, n + width) for n in range(0, N_OUT, width)]
+
         def add_bias(g):
             gate[g] = gate_pool.tile([P, PAIR, N_OUT], F32, name="gate")
             for j in range(PAIR):
-                nc.vector.tensor_tensor(out=gate[g][:, j, :], in0=acc[g, j][:], in1=bias[:], op=ALU.add)
+                for cols in pieces(g, j):
+                    nc.vector.tensor_tensor(
+                        out=gate[g][:, j, cols], in0=acc[g, j][:, cols], in1=bias[:, cols], op=ALU.add
+                    )
 
         def tanh_of_cell(g):
             tanh_c[g] = tanh_pool.tile([P, PAIR, N_OUT], F32, name="tanh_c")
@@ -143,13 +150,15 @@ def tile_ircnn_lstmcell_pb_t_kernel(
 
         def sigmoid(g):
             for j in range(PAIR):
-                nc.scalar.activation(out=gate[g][:, j, :], in_=gate[g][:, j, :], func=ACT.Sigmoid)
+                for cols in pieces(g, j):
+                    nc.scalar.activation(out=gate[g][:, j, cols], in_=gate[g][:, j, cols], func=ACT.Sigmoid)
 
         def product_and_store(g):
             for j, engine in enumerate((nc.gpsimd, nc.vector)):
-                engine.tensor_tensor(
-                    out=gate[g][:, j, :], in0=gate[g][:, j, :], in1=tanh_c[g][:, j, :], op=ALU.mult
-                )
+                for cols in pieces(g, j):
+                    engine.tensor_tensor(
+                        out=gate[g][:, j, cols], in0=gate[g][:, j, cols], in1=tanh_c[g][:, j, cols], op=ALU.mult
+                    )
                 nc.sync.dma_start(out=out_rows[:, g * PAIR + j, :], in_=gate[g][:, j, :])
 
         w_grouped = [
@@ -207,10 +216,10 @@ def tile_ircnn_lstmcell_pb_t_kernel(
                 for i in (CY, X, HX):
                     if (i, g + 1) not in codes:
                         quantise(i, g + 1)
-            if g + 3 < ROUNDS:
-                tanh_of_cell(g + 3)
             if g >= 1 and g <= ROUNDS:
                 sigmoid(g - 1)
+            if g + 3 < ROUNDS:
+                tanh_of_cell(g + 3)
             if g < ROUNDS:
                 multiply(g)
                 add_bias(g)

@@ -50,6 +50,8 @@ def tile_ircnn_lstmcell_pb_t_kernel(
         make_identity(nc, ident[:])
         ones = consts.tile([P, P], BF16)
         nc.vector.memset(ones[:], 1.0)
+        zeros = consts.tile([P, N_OUT], BF16)
+        nc.vector.memset(zeros[:], 0.0)
         bias_rows = consts.tile([P, N_OUT], BF16)
         nc.vector.memset(bias_rows[:], 0.0)
         nc.scalar.dma_start(out=bias_rows[0:1, :], in_=b_ih_o.rearrange("(o n) -> o n", o=1))
@@ -182,6 +184,12 @@ def tile_ircnn_lstmcell_pb_t_kernel(
                 in_=w_grouped[i][:].rearrange("p n t -> p (n t)"),
             )
 
+        def keep_warm(count):
+            for n in range(count):
+                idle = sums.tile([P, N_OUT], F32, name="acc")
+                nc.tensor.matmul(out=idle[:], lhsT=ones[:], rhs=zeros[:], start=True, stop=True)
+
+        keep_warm(4)
         tanh_of_cell(0)
         regroup(CY, 0, nc.vector.tensor_copy)
         bias_sum = sums.tile([P, N_OUT], F32, name="acc")
@@ -191,21 +199,26 @@ def tile_ircnn_lstmcell_pb_t_kernel(
         regroup_weights(CY, 0, nc.vector.tensor_copy)
         quantise(CY, 0)
         regroup_weights(CY, 1, nc.scalar.copy)
+        keep_warm(1)
         tanh_of_cell(1)
         regroup(CY, 1, nc.vector.tensor_copy)
         quantise_weights(CY)
         regroup_weights(X, 0, nc.vector.tensor_copy)
+        keep_warm(1)
         regroup_weights(X, 1, nc.scalar.copy)
         quantise(CY, 1)
         regroup(X, 0, nc.scalar.copy)
+        keep_warm(1)
         quantise_weights(X)
         regroup_weights(HX, 0, nc.vector.tensor_copy)
         quantise(X, 0)
         regroup_weights(HX, 1, nc.scalar.copy)
+        keep_warm(1)
         regroup(HX, 0, nc.vector.tensor_copy)
         quantise_weights(HX)
         tanh_of_cell(2)
         quantise(HX, 0)
+        keep_warm(1)
         regroup(X, 1, nc.scalar.copy)
         regroup(HX, 1, nc.vector.tensor_copy)
 

@@ -46,6 +46,10 @@ def tile_ircnn_lstmcell_pb_t_kernel(
         sums = ctx.enter_context(tc.psum_pool(name="sums", bufs=4))
         ctx.enter_context(tc.manual_schedule())
 
+        warm = consts.tile([P, 1], F32)
+        nc.vector.memset(warm[:], 0.0)
+        warm_out = consts.tile([P, 1], F32)
+        nc.scalar.activation(out=warm_out[:], in_=warm[:], func=ACT.Sigmoid)
         ident = consts.tile([P, P], F32)
         make_identity(nc, ident[:])
         ones = consts.tile([P, P], BF16)
@@ -54,12 +58,6 @@ def tile_ircnn_lstmcell_pb_t_kernel(
         nc.vector.memset(zeros[:], 0.0)
         bias_rows = consts.tile([P, N_OUT], BF16)
         nc.vector.memset(bias_rows[:], 0.0)
-        nc.scalar.dma_start(out=bias_rows[0:1, :], in_=b_ih_o.rearrange("(o n) -> o n", o=1))
-        nc.scalar.dma_start(out=bias_rows[1:2, :], in_=b_hh_o.rearrange("(o n) -> o n", o=1))
-        warm = consts.tile([P, 1], F32)
-        nc.vector.memset(warm[:], 0.0)
-        warm_out = consts.tile([P, 1], F32)
-        nc.scalar.activation(out=warm_out[:], in_=warm[:], func=ACT.Sigmoid)
 
         w_raw = [
             [resident.tile([P, PAIR, K], BF16, name="w_raw%d_%d" % (i, h)) for h in range(WEIGHT_PAIRS)]
@@ -79,6 +77,8 @@ def tile_ircnn_lstmcell_pb_t_kernel(
 
         load_rows(CY, 0)
         load_weights(CY)
+        for row, b in enumerate((b_ih_o, b_hh_o)):
+            nc.sync.dma_start(out=bias_rows[row : row + 1, :], in_=b.rearrange("(o n) -> o n", o=1))
         load_rows(CY, 1)
         load_weights(X)
         load_rows(X, 0)
@@ -192,29 +192,28 @@ def tile_ircnn_lstmcell_pb_t_kernel(
         keep_warm(4)
         tanh_of_cell(0)
         regroup(CY, 0, nc.vector.tensor_copy)
+        regroup_weights(CY, 0, nc.scalar.copy)
+        quantise(CY, 0)
+        regroup_weights(CY, 1, nc.vector.tensor_copy)
+        keep_warm(1)
+        tanh_of_cell(1)
+        regroup(CY, 1, nc.scalar.copy)
+        quantise_weights(CY)
         bias_sum = sums.tile([P, N_OUT], F32, name="acc")
         nc.tensor.matmul(out=bias_sum[:], lhsT=ones[:], rhs=bias_rows[:], start=True, stop=True)
         bias = consts.tile([P, N_OUT], F32)
         nc.vector.tensor_copy(out=bias[:], in_=bias_sum[:])
-        regroup_weights(CY, 0, nc.vector.tensor_copy)
-        quantise(CY, 0)
-        regroup_weights(CY, 1, nc.scalar.copy)
-        keep_warm(1)
-        tanh_of_cell(1)
-        regroup(CY, 1, nc.vector.tensor_copy)
-        quantise_weights(CY)
-        regroup_weights(X, 0, nc.vector.tensor_copy)
-        keep_warm(1)
-        regroup_weights(X, 1, nc.scalar.copy)
-        quantise(CY, 1)
+        regroup_weights(X, 0, nc.scalar.copy)
+        regroup_weights(X, 1, nc.vector.tensor_copy)
         regroup(X, 0, nc.scalar.copy)
         keep_warm(1)
         quantise_weights(X)
-        regroup_weights(HX, 0, nc.vector.tensor_copy)
+        regroup_weights(HX, 0, nc.scalar.copy)
         quantise(X, 0)
-        regroup_weights(HX, 1, nc.scalar.copy)
+        regroup_weights(HX, 1, nc.vector.tensor_copy)
         keep_warm(1)
-        regroup(HX, 0, nc.vector.tensor_copy)
+        regroup(HX, 0, nc.scalar.copy)
+        quantise(CY, 1)
         quantise_weights(HX)
         tanh_of_cell(2)
         quantise(HX, 0)

@@ -19,6 +19,7 @@ BATCH, K, N_OUT = 4096, 512, 512
 ROW_TILES = BATCH // P
 ROUNDS = ROW_TILES // PAIR
 WEIGHT_PAIRS = N_OUT // (PAIR * P)
+VECTOR_HELPS_EVERY = 8
 OPERANDS = 3
 X = 0
 HX = 1
@@ -156,12 +157,12 @@ def tile_ircnn_lstmcell_pb_t_kernel(
                     nc.scalar.activation(out=gate[g][:, j, cols], in_=gate[g][:, j, cols], func=ACT.Sigmoid)
 
         def product_and_store(g):
-            for j, engine in enumerate((nc.gpsimd, nc.vector)):
+            for j, engine in enumerate((nc.gpsimd if g < ROUNDS - 1 else nc.vector, nc.vector)):
                 for cols in pieces(g, j):
                     engine.tensor_tensor(
                         out=gate[g][:, j, cols], in0=gate[g][:, j, cols], in1=tanh_c[g][:, j, cols], op=ALU.mult
                     )
-                nc.sync.dma_start(out=out_rows[:, g * PAIR + j, :], in_=gate[g][:, j, :])
+                    nc.sync.dma_start(out=out_rows[:, g * PAIR + j, cols], in_=gate[g][:, j, cols])
 
         w_grouped = [
             resident.tile([P, N_OUT, PACK], BF16, name="w_grouped%d" % i, align_bytes=64) for i in range(OPERANDS)
@@ -220,6 +221,7 @@ def tile_ircnn_lstmcell_pb_t_kernel(
         keep_warm(1)
         regroup(X, 1, nc.scalar.copy)
         regroup(HX, 1, nc.vector.tensor_copy)
+        regroup(CY, 2, nc.scalar.copy)
 
         for g in range(ROUNDS + 2):
             if g >= 2:
@@ -236,6 +238,8 @@ def tile_ircnn_lstmcell_pb_t_kernel(
                 multiply(g)
                 add_bias(g)
             if g + 2 < ROUNDS:
-                regroup(CY, g + 2, nc.vector.tensor_copy)
+                vector_helps = g % VECTOR_HELPS_EVERY == 1
+                if g > 0:
+                    regroup(CY, g + 2, nc.vector.tensor_copy if g + 3 < ROUNDS else nc.scalar.copy)
                 regroup(X, g + 2, nc.scalar.copy)
-                regroup(HX, g + 2, nc.scalar.copy)
+                regroup(HX, g + 2, nc.vector.tensor_copy if vector_helps else nc.scalar.copy)

@@ -107,13 +107,13 @@ def tile_ircnn_lstmcell_pb_t_kernel(
         tanh_c = {}
 
         def regroup(i, g, copy):
-            grouped[i, g] = grouped_pool.tile([P, PAIR, P, PACK], BF16, name="grouped%d" % i, align_bytes=64)
+            grouped[i, g] = grouped_pool.tile([P, PAIR, P, PACK], BF16, name="grouped%d" % i, align_bytes=256)
             bank = transpose_pair(rows[i][g][:])
             copy(out=grouped[i, g][:].bitcast(F32), in_=bank[:].rearrange("p j u r -> p j r u"))
 
         def quantise(i, g):
-            codes[i, g] = mx_pool.tile([P, PAIR * P], U32, name="codes%d" % i, align_bytes=64)
-            scales[i, g] = mx_pool.tile([P, PAIR * P], U8, name="scales%d" % i, align_bytes=64)
+            codes[i, g] = mx_pool.tile([P, PAIR * P], U32, name="codes%d" % i, align_bytes=256)
+            scales[i, g] = mx_pool.tile([P, PAIR * P], U8, name="scales%d" % i, align_bytes=256)
             nc.vector.quantize_mx(
                 out=codes[i, g][:].bitcast(FP8X4),
                 scales=scales[i, g][:],
@@ -165,10 +165,10 @@ def tile_ircnn_lstmcell_pb_t_kernel(
                     nc.sync.dma_start(out=out_rows[:, g * PAIR + j, cols], in_=gate[g][:, j, cols])
 
         w_grouped = [
-            resident.tile([P, N_OUT, PACK], BF16, name="w_grouped%d" % i, align_bytes=64) for i in range(OPERANDS)
+            resident.tile([P, N_OUT, PACK], BF16, name="w_grouped%d" % i, align_bytes=256) for i in range(OPERANDS)
         ]
-        w_codes = [resident.tile([P, N_OUT], U32, name="w_codes%d" % i, align_bytes=64) for i in range(OPERANDS)]
-        w_scales = [resident.tile([P, N_OUT], U8, name="w_scales%d" % i, align_bytes=64) for i in range(OPERANDS)]
+        w_codes = [resident.tile([P, N_OUT], U32, name="w_codes%d" % i, align_bytes=256) for i in range(OPERANDS)]
+        w_scales = [resident.tile([P, N_OUT], U8, name="w_scales%d" % i, align_bytes=256) for i in range(OPERANDS)]
 
         def regroup_weights(i, h, copy):
             half = w_grouped[i][:].bitcast(F32)[:, h * PAIR * P : (h + 1) * PAIR * P, :]

from contextlib import ExitStack

import concourse.mybir as mybir
from concourse.masks import make_identity

F32 = mybir.dt.float32
BF16 = mybir.dt.bfloat16
U32 = mybir.dt.uint32
U8 = mybir.dt.uint8
FP8X4 = mybir.dt.float8_e4m3fn_x4
ACT = mybir.ActivationFunctionType
ALU = mybir.AluOpType

P = 128
PACK = 4
HALVES = 2
PAIR = 2
BATCH, K, N_OUT = 4096, 512, 512
ROW_TILES = BATCH // P
ROUNDS = ROW_TILES // PAIR
WEIGHT_PAIRS = N_OUT // (PAIR * P)
VECTOR_HELPS_EVERY = 8
OPERANDS = 3
X = 0
HX = 1
CY = 2

FLOPS = 2 * BATCH * K * N_OUT * OPERANDS


def tile_ircnn_lstmcell_pb_t_kernel(
    tc, x, hx, cy, w_ih_o, w_hh_o, w_po, b_ih_o, b_hh_o, out
):
    nc = tc.nc
    acts = [a.rearrange("(p t) k -> p t k", t=ROW_TILES) for a in (x, hx, cy)]
    out_rows = out.rearrange("(p t) n -> p t n", t=ROW_TILES)
    weights = [w.rearrange("(h c j) k -> h c j k", h=WEIGHT_PAIRS, j=PAIR) for w in (w_ih_o, w_hh_o, w_po)]

    with ExitStack() as ctx:
        consts = ctx.enter_context(tc.tile_pool(name="consts", bufs=1))
        resident = ctx.enter_context(tc.tile_pool(name="resident", bufs=1))
        grouped_pool = ctx.enter_context(tc.tile_pool(name="grouped", bufs=2))
        mx_pool = ctx.enter_context(tc.tile_pool(name="mx", bufs=3))
        tanh_pool = ctx.enter_context(tc.tile_pool(name="tanh", bufs=8))
        gate_pool = ctx.enter_context(tc.tile_pool(name="gate", bufs=8))
        banks = ctx.enter_context(tc.psum_pool(name="banks", bufs=4))
        sums = ctx.enter_context(tc.psum_pool(name="sums", bufs=4))
        ctx.enter_context(tc.manual_schedule())

        warm = consts.tile([P, 1], F32)
        nc.vector.memset(warm[:], 0.0)
        warm_out = consts.tile([P, 1], F32)
        nc.scalar.activation(out=warm_out[:], in_=warm[:], func=ACT.Sigmoid)
        ident = consts.tile([P, P], F32)
        make_identity(nc, ident[:])
        ones = consts.tile([P, P], BF16)
        nc.vector.memset(ones[:], 1.0)
        zeros = consts.tile([P, N_OUT], BF16)
        nc.vector.memset(zeros[:], 0.0)
        bias_rows = consts.tile([P, N_OUT], BF16)
        nc.vector.memset(bias_rows[:], 0.0)

        w_raw = [
            [resident.tile([P, PAIR, K], BF16, name="w_raw%d_%d" % (i, h)) for h in range(WEIGHT_PAIRS)]
            for i in range(OPERANDS)
        ]
        rows = [
            [resident.tile([P, PAIR, K], BF16, name="rows%d_%d" % (i, g)) for g in range(ROUNDS)]
            for i in range(OPERANDS)
        ]

        def load_rows(i, g):
            nc.sync.dma_start(out=rows[i][g][:], in_=acts[i][:, g * PAIR : (g + 1) * PAIR, :])

        def load_weights(i):
            for h in range(WEIGHT_PAIRS):
                nc.sync.dma_start(out=w_raw[i][h][:], in_=weights[i][h])

        load_rows(CY, 0)
        load_weights(CY)
        for row, b in enumerate((b_ih_o, b_hh_o)):
            nc.sync.dma_start(out=bias_rows[row : row + 1, :], in_=b.rearrange("(o n) -> o n", o=1))
        load_rows(CY, 1)
        load_weights(X)
        load_rows(X, 0)
        load_weights(HX)
        load_rows(HX, 0)
        for g in range(1, ROUNDS):
            if g + 1 < ROUNDS:
                load_rows(CY, g + 1)
            load_rows(X, g)
            load_rows(HX, g)

        def transpose_pair(rows_bf16):
            bank = banks.tile([P, PAIR, HALVES, P], F32, name="bank")
            words = rows_bf16.bitcast(F32)
            for j in range(PAIR):
                for u in range(HALVES):
                    nc.tensor.transpose(bank[:, j, u, :], words[:, j, u * P : (u + 1) * P], ident[:])
            return bank

        grouped = {}
        codes = {}
        scales = {}
        acc = {}
        gate = {}
        tanh_c = {}

        def regroup(i, g, copy):
            grouped[i, g] = grouped_pool.tile([P, PAIR, P, PACK], BF16, name="grouped%d" % i, align_bytes=256)
            bank = transpose_pair(rows[i][g][:])
            copy(out=grouped[i, g][:].bitcast(F32), in_=bank[:].rearrange("p j u r -> p j r u"))

        def quantise(i, g):
            codes[i, g] = mx_pool.tile([P, PAIR * P], U32, name="codes%d" % i, align_bytes=256)
            scales[i, g] = mx_pool.tile([P, PAIR * P], U8, name="scales%d" % i, align_bytes=256)
            nc.vector.quantize_mx(
                out=codes[i, g][:].bitcast(FP8X4),
                scales=scales[i, g][:],
                in_=grouped[i, g][:].rearrange("p j r t -> p (j r t)"),
            )

        def multiply(g):
            for j in range(PAIR):
                acc[g, j] = sums.tile([P, N_OUT], F32, name="acc")
                tile_cols = slice(j * P, (j + 1) * P)
                for i in (CY, X, HX):
                    nc.tensor.matmul_mx(
                        out=acc[g, j][:],
                        lhsT=codes[i, g][:, tile_cols].bitcast(FP8X4),
                        lhsT_scale=scales[i, g][:, tile_cols],
                        rhs=w_codes[i][:].bitcast(FP8X4),
                        rhs_scale=w_scales[i][:],
                        start=(i == CY),
                        stop=(i == HX),
                    )

        def pieces(g, j):
            width = N_OUT // 2 if (g, j) == (ROUNDS - 1, PAIR - 1) else N_OUT
            return [slice(n, n + width) for n in range(0, N_OUT, width)]

        def add_bias(g):
            gate[g] = gate_pool.tile([P, PAIR, N_OUT], F32, name="gate")
            for j in range(PAIR):
                for cols in pieces(g, j):
                    nc.vector.tensor_tensor(
                        out=gate[g][:, j, cols], in0=acc[g, j][:, cols], in1=bias[:, cols], op=ALU.add
                    )

        def tanh_of_cell(g):
            tanh_c[g] = tanh_pool.tile([P, PAIR, N_OUT], F32, name="tanh_c")
            nc.scalar.activation(out=tanh_c[g][:], in_=rows[CY][g][:], func=ACT.Tanh)

        def sigmoid(g):
            for j in range(PAIR):
                for cols in pieces(g, j):
                    nc.scalar.activation(out=gate[g][:, j, cols], in_=gate[g][:, j, cols], func=ACT.Sigmoid)

        def product_and_store(g):
            for j, engine in enumerate((nc.gpsimd if g < ROUNDS - 1 else nc.vector, nc.vector)):
                for cols in pieces(g, j):
                    engine.tensor_tensor(
                        out=gate[g][:, j, cols], in0=gate[g][:, j, cols], in1=tanh_c[g][:, j, cols], op=ALU.mult
                    )
                    nc.sync.dma_start(out=out_rows[:, g * PAIR + j, cols], in_=gate[g][:, j, cols])

        w_grouped = [
            resident.tile([P, N_OUT, PACK], BF16, name="w_grouped%d" % i, align_bytes=256) for i in range(OPERANDS)
        ]
        w_codes = [resident.tile([P, N_OUT], U32, name="w_codes%d" % i, align_bytes=256) for i in range(OPERANDS)]
        w_scales = [resident.tile([P, N_OUT], U8, name="w_scales%d" % i, align_bytes=256) for i in range(OPERANDS)]

        def regroup_weights(i, h, copy):
            half = w_grouped[i][:].bitcast(F32)[:, h * PAIR * P : (h + 1) * PAIR * P, :]
            bank = transpose_pair(w_raw[i][h][:])
            copy(
                out=half.rearrange("p (c j) u -> p c j u", j=PAIR),
                in_=bank[:].rearrange("p j u c -> p c j u"),
            )

        def quantise_weights(i):
            nc.vector.quantize_mx(
                out=w_codes[i][:].bitcast(FP8X4),
                scales=w_scales[i][:],
                in_=w_grouped[i][:].rearrange("p n t -> p (n t)"),
            )

        def keep_warm(count):
            for n in range(count):
                idle = sums.tile([P, N_OUT], F32, name="acc")
                nc.tensor.matmul(out=idle[:], lhsT=ones[:], rhs=zeros[:], start=True, stop=True)

        keep_warm(4)
        tanh_of_cell(0)
        regroup(CY, 0, nc.vector.tensor_copy)
        regroup_weights(CY, 0, nc.scalar.copy)
        quantise(CY, 0)
        regroup_weights(CY, 1, nc.vector.tensor_copy)
        keep_warm(1)
        tanh_of_cell(1)
        regroup(CY, 1, nc.scalar.copy)
        quantise_weights(CY)
        bias_sum = sums.tile([P, N_OUT], F32, name="acc")
        nc.tensor.matmul(out=bias_sum[:], lhsT=ones[:], rhs=bias_rows[:], start=True, stop=True)
        bias = consts.tile([P, N_OUT], F32)
        nc.vector.tensor_copy(out=bias[:], in_=bias_sum[:])
        regroup_weights(X, 0, nc.scalar.copy)
        regroup_weights(X, 1, nc.vector.tensor_copy)
        regroup(X, 0, nc.scalar.copy)
        keep_warm(1)
        quantise_weights(X)
        regroup_weights(HX, 0, nc.scalar.copy)
        quantise(X, 0)
        regroup_weights(HX, 1, nc.vector.tensor_copy)
        keep_warm(1)
        regroup(HX, 0, nc.scalar.copy)
        quantise(CY, 1)
        quantise_weights(HX)
        tanh_of_cell(2)
        quantise(HX, 0)
        keep_warm(1)
        regroup(X, 1, nc.scalar.copy)
        regroup(HX, 1, nc.vector.tensor_copy)
        regroup(CY, 2, nc.scalar.copy)

        for g in range(ROUNDS + 2):
            if g >= 2:
                product_and_store(g - 2)
            if g + 1 < ROUNDS:
                for i in (CY, X, HX):
                    if (i, g + 1) not in codes:
                        quantise(i, g + 1)
            if g >= 1 and g <= ROUNDS:
                sigmoid(g - 1)
            if g + 3 < ROUNDS:
                tanh_of_cell(g + 3)
            if g < ROUNDS:
                multiply(g)
                add_bias(g)
            if g + 2 < ROUNDS:
                vector_helps = g % VECTOR_HELPS_EVERY == 1
                if g > 0:
                    regroup(CY, g + 2, nc.vector.tensor_copy if g + 3 < ROUNDS else nc.scalar.copy)
                regroup(X, g + 2, nc.scalar.copy)
                regroup(HX, g + 2, nc.vector.tensor_copy if vector_helps else nc.scalar.copy)
